import numpy as np
import ml_dtypes


def mxq(x, axis, fmt="e4m3"):
    dtype, down = {"e4m3": (ml_dtypes.float8_e4m3fn, 7), "e5m2": (ml_dtypes.float8_e5m2, 14)}[fmt]
    v = np.moveaxis(np.asarray(x, np.float32).astype(ml_dtypes.bfloat16).astype(np.float64), axis, -1)
    blocks = v.reshape(v.shape[:-1] + (-1, 32))
    amax = np.abs(blocks).max(-1, keepdims=True)
    byte = np.maximum(np.where(amax > 0, np.frexp(amax)[1] - 1 + 127, 0) - down, 1)
    scale = np.exp2(byte - 127.0)
    codes = (blocks / scale).astype(np.float32).astype(dtype).astype(np.float64)
    return np.moveaxis((codes * scale).reshape(v.shape), -1, axis)


WIDE = False


def mx_kscale(k):
    if not WIDE:
        return np.ones(k)
    levels = np.array([10, -10, 5, -5, 0])
    a = np.random.permutation(np.resize(levels, k // 512 * 4)).reshape(k // 512, 4)
    idx = np.arange(k)
    return np.exp2(a[idx // 512, idx % 128 // 32])


BF16 = ml_dtypes.bfloat16


def bf(x):
    return np.asarray(x, np.float32).astype(BF16)


def f64(x):
    return np.asarray(x).astype(np.float64)


B, D, I, O = 1024, 8, 512, 256


def setup_inputs():
    s = np.tile(mx_kscale(I), D)
    return {"x": bf(np.random.standard_normal((B, D * I)) * s),
            "W": bf(np.random.standard_normal((D * O, D * I)) / np.sqrt(I) / s[None, :])}


def reference(x, W):
    W4 = f64(W).reshape(D, O, D, I)
    Wb = np.ascontiguousarray(np.einsum('dodi->doi', W4))
    xb = f64(x).reshape(B, D, I)
    xq = mxq(xb, 2, "e4m3")
    wq = mxq(Wb, 2, "e4m3")
    out = xq.transpose(1, 0, 2) @ wq.transpose(0, 2, 1)
    return out.transpose(1, 0, 2).reshape(B, D * O)

@@ -1,0 +1,125 @@
+from contextlib import ExitStack
+
+import concourse.mybir as mybir
+from concourse.masks import make_identity
+
+F32 = mybir.dt.float32
+BF16 = mybir.dt.bfloat16
+U32 = mybir.dt.uint32
+U8 = mybir.dt.uint8
+FP8X4 = mybir.dt.float8_e4m3fn_x4
+
+P = 128
+B, D, I, O = 1024, 8, 512, 256
+NT = B // P
+FLOPS = 2 * B * D * I * O
+BYTES = B * D * I * 2 + D * O * I * 2 + B * D * O * 4
+
+PIN = True
+
+
+def tile_ensemblelinear_kernel(tc, x, W, out):
+    nc = tc.nc
+    with ExitStack() as ctx:
+        keep = ctx.enter_context(tc.tile_pool(name="keep", bufs=1))
+        xpool = ctx.enter_context(tc.tile_pool(name="xpool", bufs=NT))
+        wpool = ctx.enter_context(tc.tile_pool(name="wpool", bufs=D))
+        gpool = ctx.enter_context(tc.tile_pool(name="gpool", bufs=3))
+        opool = ctx.enter_context(tc.tile_pool(name="opool", bufs=NT))
+        tps = ctx.enter_context(tc.psum_pool(name="tps", bufs=4))
+        aps = ctx.enter_context(tc.psum_pool(name="aps", bufs=4))
+        if PIN:
+            ctx.enter_context(tc.manual_schedule())
+
+        x_v = x.rearrange("(p t) k -> p t k", t=NT)
+        out_v = out.rearrange("(p t) n -> p t n", t=NT)
+
+        w_sb = []
+        for d in range(D):
+            wt = wpool.tile([P, 2 * I], BF16, name="w_raw", tag="w_raw")
+            nc.sync.dma_start(
+                out=wt[:].rearrange("p (h k) -> p h k", h=2),
+                in_=W[O * d : O * (d + 1), I * d : I * (d + 1)].rearrange("(h p) k -> p h k", p=P),
+            )
+            w_sb.append(wt)
+        x_sb = []
+        for i in range(NT):
+            xt = xpool.tile([P, D * I], BF16, name="x_raw", tag="x_raw")
+            nc.sync.dma_start(out=xt[:], in_=x_v[:, i, :])
+            x_sb.append(xt)
+
+        ident = keep.tile([P, P], F32, name="ident")
+        make_identity(nc, ident[:])
+
+        def flip(src_words, first_word, step, dst_bf16, engine):
+            bank = tps.tile([P, 2, 2 * P], F32, name="flip_bank", tag="flip_bank")
+            for c in range(2):
+                for u in range(2):
+                    col = first_word + step[c][u]
+                    nc.tensor.transpose(bank[:, u, P * c : P * (c + 1)], src_words[:, col : col + P], ident[:])
+            dst = dst_bf16.bitcast(F32).rearrange("p (c u) -> p c u", u=2)
+            src = bank[:].rearrange("p u c -> p c u")
+            if engine == "v":
+                nc.vector.tensor_copy(out=dst, in_=src)
+            else:
+                nc.scalar.copy(out=dst, in_=src)
+
+        STEP = [[0, P], [2 * P, 3 * P]]
+
+        w_grp, w_codes, w_scales = [], [], []
+        for j in range(D // 2):
+            w_grp.append(keep.tile([P, 2048], BF16, name="w_grp%d" % j, align_bytes=64))
+            w_codes.append(keep.tile([P, 512], U32, name="w_codes%d" % j, align_bytes=64))
+            w_scales.append(keep.tile([P, 512], U8, name="w_scales%d" % j, align_bytes=64))
+
+        def quant_w(j):
+            nc.vector.quantize_mx(out=w_codes[j][:].bitcast(FP8X4), scales=w_scales[j][:], in_=w_grp[j][:])
+
+        for d in range(D):
+            j, dd = d // 2, d % 2
+            flip(w_sb[d][:].bitcast(F32), 0, STEP, w_grp[j][:, 1024 * dd : 1024 * (dd + 1)], "s" if dd == 0 else "v")
+            if dd == 1 and j >= 1:
+                quant_w(j - 1)
+        quant_w(D // 2 - 1)
+
+        grp, codes, scales = {}, {}, {}
+
+        def flip_x(i):
+            grp[i] = gpool.tile([P, D * I], BF16, name="x_grp", tag="x_grp", align_bytes=64)
+            xw = x_sb[i][:].bitcast(F32)
+            for j in range(4):
+                flip(xw, 512 * j, STEP, grp[i][:, 1024 * j : 1024 * (j + 1)], "v" if j == 3 else "s")
+
+        def quant_x(i):
+            codes[i] = gpool.tile([P, D * P], U32, name="x_codes", tag="x_codes", align_bytes=64)
+            scales[i] = gpool.tile([P, D * P], U8, name="x_scales", tag="x_scales", align_bytes=64)
+            nc.vector.quantize_mx(out=codes[i][:].bitcast(FP8X4), scales=scales[i][:], in_=grp[i][:])
+
+        def multiply(i):
+            res = opool.tile([P, D * O], F32, name="res", tag="res")
+            for j in range(4):
+                acc = aps.tile([P, 2 * O], F32, name="acc", tag="acc")
+                for dd in range(2):
+                    d = 2 * j + dd
+                    nc.tensor.matmul_mx(
+                        out=acc[:, O * dd : O * (dd + 1)],
+                        lhsT=codes[i][:, P * d : P * (d + 1)].bitcast(FP8X4),
+                        lhsT_scale=scales[i][:, P * d : P * (d + 1)],
+                        rhs=w_codes[j][:, O * dd : O * (dd + 1)].bitcast(FP8X4),
+                        rhs_scale=w_scales[j][:, O * dd : O * (dd + 1)],
+                        start=True,
+                        stop=True,
+                    )
+                dst = res[:, 512 * j : 512 * (j + 1)]
+                if j % 2 == 0:
+                    nc.vector.tensor_copy(out=dst, in_=acc[:])
+                else:
+                    nc.scalar.copy(out=dst, in_=acc[:])
+            nc.sync.dma_start(out=out_v[:, i, :], in_=res[:])
+
+        flip_x(0)
+        for i in range(NT):
+            quant_x(i)
+            if i + 1 < NT:
+                flip_x(i + 1)
+            multiply(i)

@@ -16,16 +16,16 @@ FLOPS = 2 * B * D * I * O
 BYTES = B * D * I * 2 + D * O * I * 2 + B * D * O * 4
 
 PIN = True
+X_CHUNKS = [(0, 1), (1, 1), (2, 2), (4, 2), (6, 2)]
+OUT_CHUNKS = [(0, 2), (2, 2), (4, 2), (6, 1), (7, 1)]
 
 
 def tile_ensemblelinear_kernel(tc, x, W, out):
     nc = tc.nc
     with ExitStack() as ctx:
         keep = ctx.enter_context(tc.tile_pool(name="keep", bufs=1))
-        xpool = ctx.enter_context(tc.tile_pool(name="xpool", bufs=NT))
         wpool = ctx.enter_context(tc.tile_pool(name="wpool", bufs=D))
         gpool = ctx.enter_context(tc.tile_pool(name="gpool", bufs=3))
-        opool = ctx.enter_context(tc.tile_pool(name="opool", bufs=NT))
         tps = ctx.enter_context(tc.psum_pool(name="tps", bufs=4))
         aps = ctx.enter_context(tc.psum_pool(name="aps", bufs=4))
         if PIN:
@@ -42,11 +42,18 @@ def tile_ensemblelinear_kernel(tc, x, W, out):
                 in_=W[O * d : O * (d + 1), I * d : I * (d + 1)].rearrange("(h p) k -> p h k", p=P),
             )
             w_sb.append(wt)
-        x_sb = []
-        for i in range(NT):
-            xt = xpool.tile([P, D * I], BF16, name="x_raw", tag="x_raw")
-            nc.sync.dma_start(out=xt[:], in_=x_v[:, i, :])
-            x_sb.append(xt)
+        x_sb = {}
+        for first, n in X_CHUNKS:
+            xt = keep.tile([P, n * D * I], BF16, name="x_raw%d" % first)
+            nc.sync.dma_start(out=xt[:].rearrange("p (t k) -> p t k", t=n), in_=x_v[:, first : first + n, :])
+            for t in range(n):
+                x_sb[first + t] = xt[:, D * I * t : D * I * (t + 1)]
+        res_sb, res_store = {}, {}
+        for first, n in OUT_CHUNKS:
+            rt = keep.tile([P, n * D * O], F32, name="res%d" % first)
+            for t in range(n):
+                res_sb[first + t] = rt[:, D * O * t : D * O * (t + 1)]
+            res_store[first + n - 1] = (rt, first, n)
 
         ident = keep.tile([P, P], F32, name="ident")
         make_identity(nc, ident[:])
@@ -86,7 +93,7 @@ def tile_ensemblelinear_kernel(tc, x, W, out):
 
         def flip_x(i):
             grp[i] = gpool.tile([P, D * I], BF16, name="x_grp", tag="x_grp", align_bytes=64)
-            xw = x_sb[i][:].bitcast(F32)
+            xw = x_sb[i].bitcast(F32)
             for j in range(4):
                 flip(xw, 512 * j, STEP, grp[i][:, 1024 * j : 1024 * (j + 1)], "v" if j == 3 else "s")
 
@@ -96,7 +103,7 @@ def tile_ensemblelinear_kernel(tc, x, W, out):
             nc.vector.quantize_mx(out=codes[i][:].bitcast(FP8X4), scales=scales[i][:], in_=grp[i][:])
 
         def multiply(i):
-            res = opool.tile([P, D * O], F32, name="res", tag="res")
+            res = res_sb[i]
             for j in range(4):
                 acc = aps.tile([P, 2 * O], F32, name="acc", tag="acc")
                 for dd in range(2):
@@ -115,7 +122,9 @@ def tile_ensemblelinear_kernel(tc, x, W, out):
                     nc.vector.tensor_copy(out=dst, in_=acc[:])
                 else:
                     nc.scalar.copy(out=dst, in_=acc[:])
-            nc.sync.dma_start(out=out_v[:, i, :], in_=res[:])
+            if i in res_store:
+                rt, first, n = res_store[i]
+                nc.sync.dma_start(out=out_v[:, first : first + n, :], in_=rt[:].rearrange("p (t n) -> p t n", t=n))
 
         flip_x(0)
         for i in range(NT):

@@ -12,12 +12,13 @@ FP8X4 = mybir.dt.float8_e4m3fn_x4
 P = 128
 B, D, I, O = 1024, 8, 512, 256
 NT = B // P
+NB = 4
 FLOPS = 2 * B * D * I * O
 BYTES = B * D * I * 2 + D * O * I * 2 + B * D * O * 4
 
-PIN = True
-X_CHUNKS = [(0, 1), (1, 1), (2, 2), (4, 2), (6, 2)]
-OUT_CHUNKS = [(0, 2), (2, 2), (4, 2), (6, 1), (7, 1)]
+X_LOADS = [(1, 1), (2, 1), (3, 1), (4, 2), (6, 2)]
+OUT_STORES = [(0, 2), (2, 2), (4, 1), (5, 1), (6, 1)]
+W_ON_VECTOR = (1, 3, 5)
 
 
 def tile_ensemblelinear_kernel(tc, x, W, out):
@@ -26,55 +27,75 @@ def tile_ensemblelinear_kernel(tc, x, W, out):
         keep = ctx.enter_context(tc.tile_pool(name="keep", bufs=1))
         wpool = ctx.enter_context(tc.tile_pool(name="wpool", bufs=D))
         gpool = ctx.enter_context(tc.tile_pool(name="gpool", bufs=3))
-        tps = ctx.enter_context(tc.psum_pool(name="tps", bufs=4))
-        aps = ctx.enter_context(tc.psum_pool(name="aps", bufs=4))
-        if PIN:
-            ctx.enter_context(tc.manual_schedule())
+        tps = ctx.enter_context(tc.psum_pool(name="tps", bufs=NB))
+        aps = ctx.enter_context(tc.psum_pool(name="aps", bufs=NB))
+        ctx.enter_context(tc.manual_schedule())
 
         x_v = x.rearrange("(p t) k -> p t k", t=NT)
         out_v = out.rearrange("(p t) n -> p t n", t=NT)
 
-        w_sb = []
+        x_words = {}
+
+        def load_x(first, n):
+            raw = keep.tile([P, n * D * I], BF16, name="x_raw%d" % first)
+            nc.sync.dma_start(out=raw[:].rearrange("p (t k) -> p t k", t=n), in_=x_v[:, first : first + n, :])
+            for t in range(n):
+                x_words[first + t] = raw[:, D * I * t : D * I * (t + 1)].bitcast(F32)
+
+        load_x(0, 1)
+        w_words = []
         for d in range(D):
-            wt = wpool.tile([P, 2 * I], BF16, name="w_raw", tag="w_raw")
+            raw_w = wpool.tile([P, 2 * I], BF16, name="w_raw", tag="w_raw")
             nc.sync.dma_start(
-                out=wt[:].rearrange("p (h k) -> p h k", h=2),
+                out=raw_w[:].rearrange("p (h k) -> p h k", h=2),
                 in_=W[O * d : O * (d + 1), I * d : I * (d + 1)].rearrange("(h p) k -> p h k", p=P),
             )
-            w_sb.append(wt)
-        x_sb = {}
-        for first, n in X_CHUNKS:
-            xt = keep.tile([P, n * D * I], BF16, name="x_raw%d" % first)
-            nc.sync.dma_start(out=xt[:].rearrange("p (t k) -> p t k", t=n), in_=x_v[:, first : first + n, :])
+            w_words.append(raw_w[:].bitcast(F32))
+        for first, n in X_LOADS:
+            load_x(first, n)
+
+        res, res_store = {}, {}
+        for first, n in OUT_STORES + [(NT - 1, 1)]:
+            res_tile = keep.tile([P, n * D * O], F32, name="res%d" % first)
             for t in range(n):
-                x_sb[first + t] = xt[:, D * I * t : D * I * (t + 1)]
-        res_sb, res_store = {}, {}
-        for first, n in OUT_CHUNKS:
-            rt = keep.tile([P, n * D * O], F32, name="res%d" % first)
-            for t in range(n):
-                res_sb[first + t] = rt[:, D * O * t : D * O * (t + 1)]
-            res_store[first + n - 1] = (rt, first, n)
+                res[first + t] = res_tile[:, D * O * t : D * O * (t + 1)]
+            res_store[first + n - 1] = (res_tile, first, n)
 
         ident = keep.tile([P, P], F32, name="ident")
         make_identity(nc, ident[:])
 
-        def flip(src_words, first_word, step, dst_bf16, engine):
-            bank = tps.tile([P, 2, 2 * P], F32, name="flip_bank", tag="flip_bank")
-            for c in range(2):
-                for u in range(2):
-                    col = first_word + step[c][u]
-                    nc.tensor.transpose(bank[:, u, P * c : P * (c + 1)], src_words[:, col : col + P], ident[:])
-            dst = dst_bf16.bitcast(F32).rearrange("p (c u) -> p c u", u=2)
-            src = bank[:].rearrange("p u c -> p c u")
-            if engine == "v":
+        def copy(on_vector, dst, src):
+            if on_vector:
                 nc.vector.tensor_copy(out=dst, in_=src)
             else:
                 nc.scalar.copy(out=dst, in_=src)
 
-        STEP = [[0, P], [2 * P, 3 * P]]
+        def flip(words, first):
+            bank = tps.tile([P, 2, 2 * P], F32, name="flip_bank", tag="flip_bank")
+            for c in range(2):
+                for u in range(2):
+                    col = first + 2 * P * c + P * u
+                    nc.tensor.transpose(bank[:, u, P * c : P * (c + 1)], words[:, col : col + P], ident[:])
+            return bank
+
+        def regroup(bank, dst_bf16, on_vector):
+            copy(on_vector, dst_bf16.bitcast(F32).rearrange("p (c u) -> p c u", u=2), bank[:].rearrange("p u c -> p c u"))
+
+        grp, codes, scales = {}, {}, {}
+
+        def flip_x(i):
+            grp[i] = gpool.tile([P, D * I], BF16, name="x_grp", tag="x_grp", align_bytes=64)
+            banks = [flip(x_words[i], 4 * P * j) for j in range(NB)]
+            for j in range(NB):
+                regroup(banks[j], grp[i][:, 1024 * j : 1024 * (j + 1)], j < 2)
+
+        def quant_x(i):
+            codes[i] = gpool.tile([P, D * P], U32, name="x_codes", tag="x_codes", align_bytes=64)
+            scales[i] = gpool.tile([P, D * P], U8, name="x_scales", tag="x_scales", align_bytes=64)
+            nc.vector.quantize_mx(out=codes[i][:].bitcast(FP8X4), scales=scales[i][:], in_=grp[i][:])
 
         w_grp, w_codes, w_scales = [], [], []
-        for j in range(D // 2):
+        for j in range(NB):
             w_grp.append(keep.tile([P, 2048], BF16, name="w_grp%d" % j, align_bytes=64))
             w_codes.append(keep.tile([P, 512], U32, name="w_codes%d" % j, align_bytes=64))
             w_scales.append(keep.tile([P, 512], U8, name="w_scales%d" % j, align_bytes=64))
@@ -82,29 +103,9 @@ def tile_ensemblelinear_kernel(tc, x, W, out):
         def quant_w(j):
             nc.vector.quantize_mx(out=w_codes[j][:].bitcast(FP8X4), scales=w_scales[j][:], in_=w_grp[j][:])
 
-        for d in range(D):
-            j, dd = d // 2, d % 2
-            flip(w_sb[d][:].bitcast(F32), 0, STEP, w_grp[j][:, 1024 * dd : 1024 * (dd + 1)], "s" if dd == 0 else "v")
-            if dd == 1 and j >= 1:
-                quant_w(j - 1)
-        quant_w(D // 2 - 1)
-
-        grp, codes, scales = {}, {}, {}
-
-        def flip_x(i):
-            grp[i] = gpool.tile([P, D * I], BF16, name="x_grp", tag="x_grp", align_bytes=64)
-            xw = x_sb[i].bitcast(F32)
-            for j in range(4):
-                flip(xw, 512 * j, STEP, grp[i][:, 1024 * j : 1024 * (j + 1)], "v" if j == 3 else "s")
-
-        def quant_x(i):
-            codes[i] = gpool.tile([P, D * P], U32, name="x_codes", tag="x_codes", align_bytes=64)
-            scales[i] = gpool.tile([P, D * P], U8, name="x_scales", tag="x_scales", align_bytes=64)
-            nc.vector.quantize_mx(out=codes[i][:].bitcast(FP8X4), scales=scales[i][:], in_=grp[i][:])
-
-        def multiply(i):
-            res = res_sb[i]
-            for j in range(4):
+        def passes(i):
+            banks = []
+            for j in range(NB):
                 acc = aps.tile([P, 2 * O], F32, name="acc", tag="acc")
                 for dd in range(2):
                     d = 2 * j + dd
@@ -117,18 +118,48 @@ def tile_ensemblelinear_kernel(tc, x, W, out):
                         start=True,
                         stop=True,
                     )
-                dst = res[:, 512 * j : 512 * (j + 1)]
-                if j % 2 == 0:
-                    nc.vector.tensor_copy(out=dst, in_=acc[:])
-                else:
-                    nc.scalar.copy(out=dst, in_=acc[:])
+                banks.append(acc)
+            return banks
+
+        def drain(i, banks, js, on_vector):
+            for j in js:
+                copy(on_vector, res[i][:, 512 * j : 512 * (j + 1)], banks[j][:])
+
+        def store(i):
             if i in res_store:
-                rt, first, n = res_store[i]
-                nc.sync.dma_start(out=out_v[:, first : first + n, :], in_=rt[:].rearrange("p (t n) -> p t n", t=n))
+                res_tile, first, n = res_store[i]
+                nc.sync.dma_start(
+                    out=out_v[:, first : first + n, :], in_=res_tile[:].rearrange("p (t n) -> p t n", t=n)
+                )
 
         flip_x(0)
-        for i in range(NT):
-            quant_x(i)
-            if i + 1 < NT:
-                flip_x(i + 1)
-            multiply(i)
+        quant_x(0)
+        for d in range(D):
+            j, dd = d // 2, d % 2
+            regroup(flip(w_words[d], 0), w_grp[j][:, 1024 * dd : 1024 * (dd + 1)], d in W_ON_VECTOR)
+            if dd == 1 and j >= 1:
+                quant_w(j - 1)
+        quant_w(NB - 1)
+        banks = passes(0)
+        drain(0, banks, (0, 1), False)
+        drain(0, banks, (2, 3), True)
+        flip_x(1)
+        quant_x(1)
+        flip_x(2)
+
+        for i in range(1, NT - 1):
+            quant_x(i + 1)
+            banks = passes(i)
+            drain(i, banks, (0, 1, 2), False)
+            if i + 2 < NT:
+                flip_x(i + 2)
+            drain(i, banks, (3,), True)
+            store(i)
+
+        last = NT - 1
+        banks = passes(last)
+        for half in range(2):
+            drain(last, banks, (2 * half,), False)
+            drain(last, banks, (2 * half + 1,), True)
+            cols = slice(1024 * half, 1024 * (half + 1))
+            nc.sync.dma_start(out=out_v[:, last, cols], in_=res[last][:, cols])

@@ -16,9 +16,7 @@ NB = 4
 FLOPS = 2 * B * D * I * O
 BYTES = B * D * I * 2 + D * O * I * 2 + B * D * O * 4
 
-X_LOADS = [(1, 1), (2, 1), (3, 1), (4, 2), (6, 2)]
-OUT_STORES = [(0, 2), (2, 2), (4, 1), (5, 1), (6, 1)]
-W_ON_VECTOR = (1, 3, 5)
+X_PIECES = [4, 2, 1, 1, 1, 1, 1, 1]
 
 
 def tile_ensemblelinear_kernel(tc, x, W, out):
@@ -27,6 +25,7 @@ def tile_ensemblelinear_kernel(tc, x, W, out):
         keep = ctx.enter_context(tc.tile_pool(name="keep", bufs=1))
         wpool = ctx.enter_context(tc.tile_pool(name="wpool", bufs=D))
         gpool = ctx.enter_context(tc.tile_pool(name="gpool", bufs=3))
+        opool = ctx.enter_context(tc.tile_pool(name="opool", bufs=NT))
         tps = ctx.enter_context(tc.psum_pool(name="tps", bufs=NB))
         aps = ctx.enter_context(tc.psum_pool(name="aps", bufs=NB))
         ctx.enter_context(tc.manual_schedule())
@@ -34,15 +33,6 @@ def tile_ensemblelinear_kernel(tc, x, W, out):
         x_v = x.rearrange("(p t) k -> p t k", t=NT)
         out_v = out.rearrange("(p t) n -> p t n", t=NT)
 
-        x_words = {}
-
-        def load_x(first, n):
-            raw = keep.tile([P, n * D * I], BF16, name="x_raw%d" % first)
-            nc.sync.dma_start(out=raw[:].rearrange("p (t k) -> p t k", t=n), in_=x_v[:, first : first + n, :])
-            for t in range(n):
-                x_words[first + t] = raw[:, D * I * t : D * I * (t + 1)].bitcast(F32)
-
-        load_x(0, 1)
         w_words = []
         for d in range(D):
             raw_w = wpool.tile([P, 2 * I], BF16, name="w_raw", tag="w_raw")
@@ -51,48 +41,32 @@ def tile_ensemblelinear_kernel(tc, x, W, out):
                 in_=W[O * d : O * (d + 1), I * d : I * (d + 1)].rearrange("(h p) k -> p h k", p=P),
             )
             w_words.append(raw_w[:].bitcast(F32))
-        for first, n in X_LOADS:
-            load_x(first, n)
-
-        res, res_store = {}, {}
-        for first, n in OUT_STORES + [(NT - 1, 1)]:
-            res_tile = keep.tile([P, n * D * O], F32, name="res%d" % first)
-            for t in range(n):
-                res[first + t] = res_tile[:, D * O * t : D * O * (t + 1)]
-            res_store[first + n - 1] = (res_tile, first, n)
+        x_src = {}
+        for i in range(NT):
+            n = X_PIECES[i]
+            width = D * I // n
+            for c in range(n):
+                raw_x = keep.tile([P, width], BF16, name="x_raw%d_%d" % (i, c))
+                nc.sync.dma_start(out=raw_x[:], in_=x_v[:, i, width * c : width * (c + 1)])
+                for b in range(NB // n):
+                    x_src[(i, c * (NB // n) + b)] = (raw_x[:].bitcast(F32), 4 * P * b)
 
         ident = keep.tile([P, P], F32, name="ident")
         make_identity(nc, ident[:])
 
-        def copy(on_vector, dst, src):
-            if on_vector:
+        def copy(engine, dst, src):
+            if engine == "v":
                 nc.vector.tensor_copy(out=dst, in_=src)
             else:
                 nc.scalar.copy(out=dst, in_=src)
 
-        def flip(words, first):
+        def flip(words, first, dst_bf16, engine):
             bank = tps.tile([P, 2, 2 * P], F32, name="flip_bank", tag="flip_bank")
             for c in range(2):
                 for u in range(2):
                     col = first + 2 * P * c + P * u
                     nc.tensor.transpose(bank[:, u, P * c : P * (c + 1)], words[:, col : col + P], ident[:])
-            return bank
-
-        def regroup(bank, dst_bf16, on_vector):
-            copy(on_vector, dst_bf16.bitcast(F32).rearrange("p (c u) -> p c u", u=2), bank[:].rearrange("p u c -> p c u"))
-
-        grp, codes, scales = {}, {}, {}
-
-        def flip_x(i):
-            grp[i] = gpool.tile([P, D * I], BF16, name="x_grp", tag="x_grp", align_bytes=64)
-            banks = [flip(x_words[i], 4 * P * j) for j in range(NB)]
-            for j in range(NB):
-                regroup(banks[j], grp[i][:, 1024 * j : 1024 * (j + 1)], j < 2)
-
-        def quant_x(i):
-            codes[i] = gpool.tile([P, D * P], U32, name="x_codes", tag="x_codes", align_bytes=64)
-            scales[i] = gpool.tile([P, D * P], U8, name="x_scales", tag="x_scales", align_bytes=64)
-            nc.vector.quantize_mx(out=codes[i][:].bitcast(FP8X4), scales=scales[i][:], in_=grp[i][:])
+            copy(engine, dst_bf16.bitcast(F32).rearrange("p (c u) -> p c u", u=2), bank[:].rearrange("p u c -> p c u"))
 
         w_grp, w_codes, w_scales = [], [], []
         for j in range(NB):
@@ -103,8 +77,34 @@ def tile_ensemblelinear_kernel(tc, x, W, out):
         def quant_w(j):
             nc.vector.quantize_mx(out=w_codes[j][:].bitcast(FP8X4), scales=w_scales[j][:], in_=w_grp[j][:])
 
-        def passes(i):
-            banks = []
+        for d in range(D):
+            j, dd = d // 2, d % 2
+            flip(w_words[d], 0, w_grp[j][:, 1024 * dd : 1024 * (dd + 1)], "s" if dd == 0 else "v")
+            if dd == 1 and j >= 1:
+                quant_w(j - 1)
+        quant_w(NB - 1)
+
+        grp, codes, scales = {}, {}, {}
+
+        def flip_x(i, engines):
+            grp[i] = gpool.tile([P, D * I], BF16, name="x_grp", tag="x_grp", align_bytes=64)
+            for j in range(NB):
+                words, first = x_src[(i, j)]
+                flip(words, first, grp[i][:, 1024 * j : 1024 * (j + 1)], engines[j])
+
+        def quant_x(i, parts):
+            codes[i] = gpool.tile([P, D * P], U32, name="x_codes", tag="x_codes", align_bytes=64)
+            scales[i] = gpool.tile([P, D * P], U8, name="x_scales", tag="x_scales", align_bytes=64)
+            w = D * P // parts
+            for c in range(parts):
+                nc.vector.quantize_mx(
+                    out=codes[i][:, w * c : w * (c + 1)].bitcast(FP8X4),
+                    scales=scales[i][:, w * c : w * (c + 1)],
+                    in_=grp[i][:, 4 * w * c : 4 * w * (c + 1)],
+                )
+
+        def multiply(i, engines, stores):
+            res = opool.tile([P, D * O], F32, name="res", tag="res")
             for j in range(NB):
                 acc = aps.tile([P, 2 * O], F32, name="acc", tag="acc")
                 for dd in range(2):
@@ -118,48 +118,19 @@ def tile_ensemblelinear_kernel(tc, x, W, out):
                         start=True,
                         stop=True,
                     )
-                banks.append(acc)
-            return banks
+                copy(engines[j], res[:, 512 * j : 512 * (j + 1)], acc[:])
+                per = NB // stores
+                if j % per == per - 1:
+                    cols = slice(512 * (j + 1 - per), 512 * (j + 1))
+                    nc.sync.dma_start(out=out_v[:, i, cols], in_=res[:, cols])
 
-        def drain(i, banks, js, on_vector):
-            for j in js:
-                copy(on_vector, res[i][:, 512 * j : 512 * (j + 1)], banks[j][:])
-
-        def store(i):
-            if i in res_store:
-                res_tile, first, n = res_store[i]
-                nc.sync.dma_start(
-                    out=out_v[:, first : first + n, :], in_=res_tile[:].rearrange("p (t n) -> p t n", t=n)
-                )
-
-        flip_x(0)
-        quant_x(0)
-        for d in range(D):
-            j, dd = d // 2, d % 2
-            regroup(flip(w_words[d], 0), w_grp[j][:, 1024 * dd : 1024 * (dd + 1)], d in W_ON_VECTOR)
-            if dd == 1 and j >= 1:
-                quant_w(j - 1)
-        quant_w(NB - 1)
-        banks = passes(0)
-        drain(0, banks, (0, 1), False)
-        drain(0, banks, (2, 3), True)
-        flip_x(1)
-        quant_x(1)
-        flip_x(2)
-
-        for i in range(1, NT - 1):
-            quant_x(i + 1)
-            banks = passes(i)
-            drain(i, banks, (0, 1, 2), False)
-            if i + 2 < NT:
-                flip_x(i + 2)
-            drain(i, banks, (3,), True)
-            store(i)
-
-        last = NT - 1
-        banks = passes(last)
-        for half in range(2):
-            drain(last, banks, (2 * half,), False)
-            drain(last, banks, (2 * half + 1,), True)
-            cols = slice(1024 * half, 1024 * (half + 1))
-            nc.sync.dma_start(out=out_v[:, last, cols], in_=res[last][:, cols])
+        flip_x(0, "sssv")
+        for i in range(NT - 2):
+            quant_x(i, 1)
+            flip_x(i + 1, "sssv")
+            multiply(i, "vsvs", 1)
+        quant_x(NT - 2, 1)
+        flip_x(NT - 1, "svsv")
+        quant_x(NT - 1, 2)
+        multiply(NT - 2, "sssv", 1)
+        multiply(NT - 1, "svsv", 2)

from contextlib import ExitStack

import concourse.mybir as mybir
from concourse.masks import make_identity

F32 = mybir.dt.float32
BF16 = mybir.dt.bfloat16
U32 = mybir.dt.uint32
U8 = mybir.dt.uint8
FP8X4 = mybir.dt.float8_e4m3fn_x4

P = 128
B, D, I, O = 1024, 8, 512, 256
NT = B // P
NB = 4
FLOPS = 2 * B * D * I * O
BYTES = B * D * I * 2 + D * O * I * 2 + B * D * O * 4

X_PIECES = [4, 2, 1, 1, 1, 1, 1, 1]


def tile_ensemblelinear_kernel(tc, x, W, out):
    nc = tc.nc
    with ExitStack() as ctx:
        keep = ctx.enter_context(tc.tile_pool(name="keep", bufs=1))
        wpool = ctx.enter_context(tc.tile_pool(name="wpool", bufs=D))
        gpool = ctx.enter_context(tc.tile_pool(name="gpool", bufs=3))
        opool = ctx.enter_context(tc.tile_pool(name="opool", bufs=NT))
        tps = ctx.enter_context(tc.psum_pool(name="tps", bufs=NB))
        aps = ctx.enter_context(tc.psum_pool(name="aps", bufs=NB))
        ctx.enter_context(tc.manual_schedule())

        x_v = x.rearrange("(p t) k -> p t k", t=NT)
        out_v = out.rearrange("(p t) n -> p t n", t=NT)

        w_words = []
        for d in range(D):
            raw_w = wpool.tile([P, 2 * I], BF16, name="w_raw", tag="w_raw")
            nc.sync.dma_start(
                out=raw_w[:].rearrange("p (h k) -> p h k", h=2),
                in_=W[O * d : O * (d + 1), I * d : I * (d + 1)].rearrange("(h p) k -> p h k", p=P),
            )
            w_words.append(raw_w[:].bitcast(F32))
        x_src = {}
        for i in range(NT):
            n = X_PIECES[i]
            width = D * I // n
            for c in range(n):
                raw_x = keep.tile([P, width], BF16, name="x_raw%d_%d" % (i, c))
                nc.sync.dma_start(out=raw_x[:], in_=x_v[:, i, width * c : width * (c + 1)])
                for b in range(NB // n):
                    x_src[(i, c * (NB // n) + b)] = (raw_x[:].bitcast(F32), 4 * P * b)

        ident = keep.tile([P, P], F32, name="ident")
        make_identity(nc, ident[:])

        def copy(engine, dst, src):
            if engine == "v":
                nc.vector.tensor_copy(out=dst, in_=src)
            else:
                nc.scalar.copy(out=dst, in_=src)

        def flip(words, first, dst_bf16, engine):
            bank = tps.tile([P, 2, 2 * P], F32, name="flip_bank", tag="flip_bank")
            for c in range(2):
                for u in range(2):
                    col = first + 2 * P * c + P * u
                    nc.tensor.transpose(bank[:, u, P * c : P * (c + 1)], words[:, col : col + P], ident[:])
            copy(engine, dst_bf16.bitcast(F32).rearrange("p (c u) -> p c u", u=2), bank[:].rearrange("p u c -> p c u"))

        w_grp, w_codes, w_scales = [], [], []
        for j in range(NB):
            w_grp.append(keep.tile([P, 2048], BF16, name="w_grp%d" % j, align_bytes=64))
            w_codes.append(keep.tile([P, 512], U32, name="w_codes%d" % j, align_bytes=64))
            w_scales.append(keep.tile([P, 512], U8, name="w_scales%d" % j, align_bytes=64))

        def quant_w(j):
            nc.vector.quantize_mx(out=w_codes[j][:].bitcast(FP8X4), scales=w_scales[j][:], in_=w_grp[j][:])

        for d in range(D):
            j, dd = d // 2, d % 2
            flip(w_words[d], 0, w_grp[j][:, 1024 * dd : 1024 * (dd + 1)], "s" if dd == 0 else "v")
            if dd == 1 and j >= 1:
                quant_w(j - 1)
        quant_w(NB - 1)

        grp, codes, scales = {}, {}, {}

        def flip_x(i, engines):
            grp[i] = gpool.tile([P, D * I], BF16, name="x_grp", tag="x_grp", align_bytes=64)
            for j in range(NB):
                words, first = x_src[(i, j)]
                flip(words, first, grp[i][:, 1024 * j : 1024 * (j + 1)], engines[j])

        def quant_x(i, parts):
            codes[i] = gpool.tile([P, D * P], U32, name="x_codes", tag="x_codes", align_bytes=64)
            scales[i] = gpool.tile([P, D * P], U8, name="x_scales", tag="x_scales", align_bytes=64)
            w = D * P // parts
            for c in range(parts):
                nc.vector.quantize_mx(
                    out=codes[i][:, w * c : w * (c + 1)].bitcast(FP8X4),
                    scales=scales[i][:, w * c : w * (c + 1)],
                    in_=grp[i][:, 4 * w * c : 4 * w * (c + 1)],
                )

        def multiply(i, engines, stores):
            res = opool.tile([P, D * O], F32, name="res", tag="res")
            for j in range(NB):
                acc = aps.tile([P, 2 * O], F32, name="acc", tag="acc")
                for dd in range(2):
                    d = 2 * j + dd
                    nc.tensor.matmul_mx(
                        out=acc[:, O * dd : O * (dd + 1)],
                        lhsT=codes[i][:, P * d : P * (d + 1)].bitcast(FP8X4),
                        lhsT_scale=scales[i][:, P * d : P * (d + 1)],
                        rhs=w_codes[j][:, O * dd : O * (dd + 1)].bitcast(FP8X4),
                        rhs_scale=w_scales[j][:, O * dd : O * (dd + 1)],
                        start=True,
                        stop=True,
                    )
                copy(engines[j], res[:, 512 * j : 512 * (j + 1)], acc[:])
                per = NB // stores
                if j % per == per - 1:
                    cols = slice(512 * (j + 1 - per), 512 * (j + 1))
                    nc.sync.dma_start(out=out_v[:, i, cols], in_=res[:, cols])

        flip_x(0, "sssv")
        for i in range(NT - 2):
            quant_x(i, 1)
            flip_x(i + 1, "sssv")
            multiply(i, "vsvs", 1)
        quant_x(NT - 2, 1)
        flip_x(NT - 1, "svsv")
        quant_x(NT - 1, 2)
        multiply(NT - 2, "sssv", 1)
        multiply(NT - 1, "svsv", 2)
